import numpy as np
import ml_dtypes


def mxq(x, axis, fmt="e4m3"):
    dtype, down = {"e4m3": (ml_dtypes.float8_e4m3fn, 7), "e5m2": (ml_dtypes.float8_e5m2, 14)}[fmt]
    v = np.moveaxis(np.asarray(x, np.float32).astype(ml_dtypes.bfloat16).astype(np.float64), axis, -1)
    blocks = v.reshape(v.shape[:-1] + (-1, 32))
    amax = np.abs(blocks).max(-1, keepdims=True)
    byte = np.maximum(np.where(amax > 0, np.frexp(amax)[1] - 1 + 127, 0) - down, 1)
    scale = np.exp2(byte - 127.0)
    codes = (blocks / scale).astype(np.float32).astype(dtype).astype(np.float64)
    return np.moveaxis((codes * scale).reshape(v.shape), -1, axis)


WIDE = False


def mx_kscale(k):
    if not WIDE:
        return np.ones(k)
    levels = np.array([10, -10, 5, -5, 0])
    a = np.random.permutation(np.resize(levels, k // 512 * 4)).reshape(k // 512, 4)
    idx = np.arange(k)
    return np.exp2(a[idx // 512, idx % 128 // 32])


BF16 = ml_dtypes.bfloat16


def bf(x):
    return np.asarray(x, np.float32).astype(BF16)


def f64(x):
    return np.asarray(x).astype(np.float64)


B, H, FEAT, AUX, NS, FC, C = 1024, 1024, 128, 128, 2, 1024, 256
IN = FEAT + AUX + NS


def sigmoid(v):
    return 1.0 / (1.0 + np.exp(-v))


def setup_inputs():
    s = mx_kscale(H)
    s = s / s.max()
    col = np.concatenate([np.full(FEAT, 0.6 / np.sqrt(FEAT)), np.full(AUX, 0.6 / np.sqrt(AUX)), np.full(NS, 0.6 / np.sqrt(NS))])
    return {"x": bf(np.random.standard_normal((B, NS))),
            "feat": bf(np.random.standard_normal((B, FEAT))),
            "aux1": bf(np.random.standard_normal((B, AUX))),
            "h": bf(np.random.standard_normal((B, H)) * s),
            "w_ih": bf(np.random.standard_normal((3 * H, IN)) * col),
            "w_hh": bf(np.random.standard_normal((3 * H, H)) / np.sqrt(H) / s),
            "b_ih": bf(np.random.standard_normal(3 * H) * 0.3),
            "b_hh": bf(np.random.standard_normal(3 * H) * 0.3)}


def reference(x, feat, aux1, h, w_ih, w_hh, b_ih, b_hh):
    hh, wi, xx = f64(h), f64(w_ih), f64(x)
    gi = f64(feat) @ wi[:, :FEAT].T + f64(aux1) @ wi[:, FEAT:FEAT + AUX].T
    for j in range(NS):
        gi = gi + xx[:, j:j + 1] * wi[:, FEAT + AUX + j][None, :]
    gi = gi + f64(b_ih)
    gh = (mxq(hh, 1, "e4m3") @ mxq(f64(w_hh), 1, "e4m3").T) + f64(b_hh)
    i_r, i_z, i_n = np.split(gi, 3, axis=1)
    h_r, h_z, h_n = np.split(gh, 3, axis=1)
    r = sigmoid(i_r + h_r)
    z = sigmoid(i_z + h_z)
    n = np.tanh(i_n + r * h_n)
    return (1.0 - z) * n + z * hh

@@ -1,0 +1,388 @@
+from contextlib import ExitStack
+
+import concourse.mybir as mybir
+from concourse.masks import make_identity
+
+F32 = mybir.dt.float32
+BF16 = mybir.dt.bfloat16
+U32 = mybir.dt.uint32
+U8 = mybir.dt.uint8
+FP8X4 = mybir.dt.float8_e4m3fn_x4
+ALU = mybir.AluOpType
+AF = mybir.ActivationFunctionType
+
+P = 128
+B = 1024
+H = 1024
+IN = 258
+NB = 512
+NSLOT = 16
+OLAG = 6
+FLOPS = 2 * B * 3 * H * (H + IN)
+
+
+def weave(ms, ts):
+    gaps = len(ms) - 1
+    k = 0
+    for i, m in enumerate(ms):
+        m()
+        if i < gaps:
+            hi = ((i + 1) * len(ts) + gaps - 1) // gaps
+            while k < hi:
+                ts[k]()
+                k += 1
+
+
+def tile_wavernncell_pa_kernel(tc, x, feat, aux1, h, w_ih, w_hh, b_ih, b_hh, out):
+    nc = tc.nc
+    with ExitStack() as ctx:
+        ctx.enter_context(tc.manual_schedule())
+        const = ctx.enter_context(tc.tile_pool(name="const", bufs=1))
+        wpool = ctx.enter_context(tc.tile_pool(name="wpool", bufs=2))
+        work = ctx.enter_context(tc.tile_pool(name="work", bufs=2))
+        acc = ctx.enter_context(tc.psum_pool(name="acc", bufs=5))
+        tp = ctx.enter_context(tc.psum_pool(name="tp", bufs=3))
+
+        feat_v = feat.rearrange("(t p) k -> p t k", p=P)
+        aux_v = aux1.rearrange("(t p) k -> p t k", p=P)
+        x_v = x.rearrange("(t p) c -> p t c", p=P)
+        h_v = h.rearrange("(t p) k -> p t k", p=P)
+        out_v = out.rearrange("(t p) j -> p t j", p=P)
+        wih_v = w_ih.rearrange("(G c q e) k -> c q G (e k)", G=3, c=4, q=P, e=2)
+        whh_v = w_hh.rearrange("(G c q e) k -> c q G (e k)", G=3, c=4, q=P, e=2)
+        bih_v = b_ih.rearrange("(m q e) -> q m e", m=12, q=P, e=2)
+        bhh_v = b_hh.rearrange("(m q e) -> q m e", m=12, q=P, e=2)
+
+        ident_f = const.tile([P, P], F32, name="ident_f")
+        ident_b = const.tile([P, P], BF16, name="ident_b")
+        warm = const.tile([P, 1], F32, name="warm")
+        fn = const.tile([P, 8, P], BF16, name="fn")
+        an = const.tile([P, 8, P], BF16, name="an")
+        xn = const.tile([P, 8, P], BF16, name="xn")
+        feat_t = const.tile([P, B], BF16, name="feat_t")
+        aux_t = const.tile([P, B], BF16, name="aux_t")
+        x_t = const.tile([P, B], BF16, name="x_t")
+        xb = const.tile([P, 2 * B], BF16, name="xb")
+        hn = const.tile([P, 8, H], BF16, name="hn")
+        hg = const.tile([P, 2, B, 4], BF16, name="hg", align_bytes=64)
+        hc = const.tile([P, 2, B], U32, name="hc", align_bytes=64)
+        hs = const.tile([P, 2, B], U8, name="hs", align_bytes=64)
+        wx = const.tile([P, 4, 3, P], BF16, name="wx")
+        bi = const.tile([P, 12, 2], BF16, name="bi")
+        bh2 = const.tile([P, 12, 2], BF16, name="bh2")
+        b_r = const.tile([P, 4, 2], F32, name="b_r")
+        b_zn = const.tile([P, 4, 2], F32, name="b_zn")
+        b_in = const.tile([P, 4, 2], F32, name="b_in")
+        b_hn = const.tile([P, 4, 2], F32, name="b_hn")
+
+        wt = {}
+        ut = {}
+        pr = {}
+        ft = {}
+
+        def load_w(c):
+            win = wpool.tile([P, 3, 2 * IN], BF16, name="win", tag="win")
+            wn = wpool.tile([P, 3, 2 * H], BF16, name="wn", tag="wn")
+            if c == 0:
+                nc.sync.dma_start(out=win[:], in_=wih_v[c])
+            for G in range(3):
+                nc.sync.dma_start(out=wn[:, G, :], in_=whh_v[c, :, G, :])
+            if c > 0:
+                nc.sync.dma_start(out=win[:], in_=wih_v[c])
+            wt[c] = {"win": win, "wn": wn}
+
+        nc.vector.memset(warm[:], 0.0)
+        nc.vector.memset(xn[:], 0.0)
+        nc.vector.memset(wx[:], 0.0)
+        make_identity(nc, ident_b[:])
+        make_identity(nc, ident_f[:])
+        nc.sync.dma_start(out=fn[:], in_=feat_v)
+        nc.sync.dma_start(out=an[:], in_=aux_v)
+        with nc.allow_non_contiguous_dma(reason="small vectors, four bytes a piece"):
+            nc.scalar.dma_start(out=xn[:, :, 0:2], in_=x_v)
+            nc.scalar.dma_start(out=bi[:], in_=bih_v)
+            nc.scalar.dma_start(out=bh2[:], in_=bhh_v)
+        nc.scalar.dma_start(out=xb[:], in_=x.rearrange("b c -> (b c)").partition_broadcast(P))
+        nc.scalar.activation(out=warm[:], in_=warm[:], func=AF.Sigmoid)
+        win0 = wpool.tile([P, 3, 2 * IN], BF16, name="win", tag="win")
+        nc.sync.dma_start(out=win0[:], in_=wih_v[0])
+        for k in range(4):
+            nc.sync.dma_start(out=hn[:, 2 * k:2 * k + 2, :], in_=h_v[:, 2 * k:2 * k + 2, :])
+        wn0 = wpool.tile([P, 3, 2 * H], BF16, name="wn", tag="wn")
+        for G in range(3):
+            nc.sync.dma_start(out=wn0[:, G, :], in_=whh_v[0, :, G, :])
+        wt[0] = {"win": win0, "wn": wn0}
+        load_w(1)
+
+        xb_v = xb[:].rearrange("p (b c) -> p b c", c=2)
+        hn_w = hn[:].bitcast(F32)
+        hg_w = hg[:].bitcast(F32)
+
+        def copy_on(eng, dst, src):
+            if eng == "act":
+                nc.scalar.copy(out=dst, in_=src)
+            else:
+                nc.vector.tensor_copy(out=dst, in_=src)
+
+        def tr(dst, src, ident):
+            return lambda: nc.tensor.transpose(dst, src, ident[:])
+
+        def job_rows(src, dst):
+            pt = tp.tile([P, 8, P], BF16, name="pt_f", tag="tp")
+            ts = [tr(pt[:, t, :], src[:, t, :], ident_b) for t in range(8)]
+            return ts, lambda eng: copy_on(eng, dst[:], pt[:].rearrange("p t b -> p (t b)"))
+
+        def job_h(t):
+            pt = tp.tile([P, 4, P], F32, name="pt_h", tag="tp")
+            ts = [tr(pt[:, wb, :], hn_w[:, t, wb * P:(wb + 1) * P], ident_f) for wb in range(4)]
+            return ts, lambda eng: copy_on(eng, hg_w[:, :, t * P:(t + 1) * P, :],
+                                           pt[:].rearrange("p (g u) b -> p g b u", g=2))
+
+        def begin_w(c):
+            w = wt[c]
+            w["w01"] = wpool.tile([P, 3, 2, 2], F32, name="w01", tag="w01")
+            w["wit"] = wpool.tile([P, 15, P], BF16, name="wit", tag="wit")
+            w["wg"] = wpool.tile([P, 6, 2, P, 4], BF16, name="wg", tag="wg", align_bytes=64)
+            w["wc"] = wpool.tile([P, 6, 2, P], U32, name="wc", tag="wc", align_bytes=64)
+            w["ws"] = wpool.tile([P, 6, 2, P], U8, name="ws", tag="ws", align_bytes=64)
+
+        def small_w(c):
+            win_v = wt[c]["win"][:].rearrange("p G (e k) -> p G e k", e=2)
+            nc.vector.tensor_copy(out=wt[c]["w01"][:], in_=win_v[:, :, :, 256:258])
+            nc.vector.tensor_copy(out=wx[:, c, 0:2, 0:2], in_=win_v[:, 0, :, 256:258])
+            nc.vector.tensor_copy(out=wx[:, c, 2, 0:2], in_=win_v[:, 1, 0, 256:258])
+
+        def job_ia(c):
+            win_v = wt[c]["win"][:].rearrange("p G (e k) -> p G e k", e=2)
+            wit = wt[c]["wit"]
+            pt = tp.tile([P, 8, P], BF16, name="pt_a", tag="tp")
+            ts = [tr(pt[:, i, :], win_v[:, i // 4, (i // 2) % 2, (i % 2) * P:(i % 2 + 1) * P], ident_b)
+                  for i in range(8)]
+            return ts, lambda eng: copy_on(eng, wit[:, 0:8, :], pt[:])
+
+        def job_ib(c):
+            win_v = wt[c]["win"][:].rearrange("p G (e k) -> p G e k", e=2)
+            wit = wt[c]["wit"]
+            pt = tp.tile([P, 8, P], BF16, name="pt_b", tag="tp")
+            ts = [tr(pt[:, i, :], win_v[:, 2, i // 2, (i % 2) * P:(i % 2 + 1) * P], ident_b) for i in range(4)]
+            ts.extend([tr(pt[:, 4 + i, :], wx[:, c, i, :], ident_b) for i in range(3)])
+            return ts, lambda eng: copy_on(eng, wit[:, 8:15, :], pt[:, 0:7, :])
+
+        def job_w(c, ge):
+            wn_w = wt[c]["wn"][:].bitcast(F32)
+            wg_w = wt[c]["wg"][:].bitcast(F32)
+            G, e = ge // 2, ge % 2
+            pt = tp.tile([P, 4, P], F32, name="pt_w", tag="tp")
+            ts = [tr(pt[:, wb, :], wn_w[:, G, e * 512 + wb * P:e * 512 + (wb + 1) * P], ident_f)
+                  for wb in range(4)]
+            return ts, lambda eng: copy_on(eng, wg_w[:, ge, :, :, :],
+                                           pt[:].rearrange("p (g u) q -> p g q u", g=2))
+
+        def quant_w(c, G):
+            w = wt[c]
+            nc.vector.quantize_mx(
+                out=w["wc"][:, 2 * G:2 * G + 2, :, :].rearrange("p a g q -> p (a g q)").bitcast(FP8X4),
+                scales=w["ws"][:, 2 * G:2 * G + 2, :, :].rearrange("p a g q -> p (a g q)"),
+                in_=w["wg"][:, 2 * G:2 * G + 2, :, :, :].rearrange("p a g q t -> p (a g q t)"))
+
+        def quant_h(g, bh):
+            bs = slice(bh * NB, (bh + 1) * NB)
+            nc.vector.quantize_mx(out=hc[:, g, bs].bitcast(FP8X4), scales=hs[:, g, bs],
+                                  in_=hg[:, g, bs, :].rearrange("p b t -> p (b t)"))
+
+        def job_o(c, i):
+            f_t = ft[c]
+            js = slice(256 * c, 256 * (c + 1))
+            pt = tp.tile([P, 2, 2, P], F32, name="pt_o", tag="tp")
+            ts = [tr(pt[:, k, e, :], f_t[:, e, (2 * i + k) * P:(2 * i + k + 1) * P], ident_f)
+                  for k in range(2) for e in range(2)]
+
+            def ev(eng):
+                o_t = work.tile([P, 2, 256], F32, name="o_t", tag="o_t", bufs=3)
+                nc.vector.tensor_tensor(out=o_t[:].rearrange("p k (q e) -> p k q e", e=2),
+                                        in0=pt[:].rearrange("p k e q -> p k q e"),
+                                        in1=hn[:, 2 * i:2 * i + 2, js].rearrange("p k (q e) -> p k q e", e=2),
+                                        op=ALU.add)
+                nc.sync.dma_start(out=out_v[:, 2 * i:2 * i + 2, js], in_=o_t[:])
+            return ts, ev
+
+        def run_job(job, eng):
+            for t in job[0]:
+                t()
+            job[1](eng)
+
+        begin_w(0)
+        run_job(job_rows(fn, feat_t), "act")
+        run_job(job_rows(an, aux_t), "dve")
+        small_w(0)
+        run_job(job_ia(0), "act")
+        run_job(job_ib(0), "dve")
+        run_job(job_rows(xn, x_t), "act")
+        for t in range(8):
+            run_job(job_h(t), "act" if t % 2 == 0 else "dve")
+            if t == 4:
+                quant_h(0, 0)
+                quant_h(1, 0)
+        for ge in range(6):
+            run_job(job_w(0, ge), "act" if ge % 2 == 0 else "dve")
+            if ge == 0:
+                quant_h(0, 1)
+                quant_h(1, 1)
+            if ge == 3:
+                quant_w(0, 0)
+            if ge == 5:
+                quant_w(0, 1)
+        quant_w(0, 2)
+        nc.vector.tensor_tensor(out=b_r[:], in0=bi[:, 0:4, :], in1=bh2[:, 0:4, :], op=ALU.add)
+        nc.vector.scalar_tensor_tensor(out=b_zn[:], in0=bi[:, 4:8, :], scalar=-1.0, in1=bh2[:, 4:8, :],
+                                       op0=ALU.mult, op1=ALU.subtract)
+        nc.vector.tensor_copy(out=b_in[:], in_=bi[:, 8:12, :])
+        nc.vector.tensor_copy(out=b_hn[:], in_=bh2[:, 8:12, :])
+
+
+        def unit_of(s):
+            return s // 4, (s // 2) % 2, s % 2
+
+        def mm(ps, lhsT, rhs, start, stop):
+            return lambda: nc.tensor.matmul(ps[:], lhsT=lhsT, rhs=rhs, start=start, stop=stop)
+
+        def pe_unit(s, ts):
+            c, bh, e = unit_of(s)
+            w = wt[c]
+            wit, wc, ws = w["wit"], w["wc"], w["ws"]
+            bs = slice(bh * NB, (bh + 1) * NB)
+            gi_r = acc.tile([P, NB], F32, name="gi_r", tag="acc")
+            gi_n = acc.tile([P, NB], F32, name="gi_n", tag="acc")
+            gi_z = acc.tile([P, NB], F32, name="gi_z", tag="acc")
+            ms = [mm(gi_r, wit[:, 2 * e, :], feat_t[:, bs], True, False),
+                  mm(gi_r, wit[:, 2 * e + 1, :], aux_t[:, bs], False, False),
+                  mm(gi_r, wit[:, 12 + e, :], x_t[:, bs], False, True),
+                  mm(gi_n, wit[:, 8 + 2 * e, :], feat_t[:, bs], True, False),
+                  mm(gi_n, wit[:, 8 + 2 * e + 1, :], aux_t[:, bs], False, True),
+                  mm(gi_z, wit[:, 4 + 2 * e, :], feat_t[:, bs], True, False),
+                  mm(gi_z, wit[:, 4 + 2 * e + 1, :], aux_t[:, bs], False, e == 1)]
+            if e == 0:
+                ms.append(mm(gi_z, wit[:, 14, :], x_t[:, bs], False, True))
+            weave(ms, ts)
+            gh = {}
+            for G in (0, 1, 2):
+                ps = acc.tile([P, NB], F32, name="gh%d" % G, tag="acc")
+                for kg in range(2):
+                    nc.tensor.matmul_mx(ps[:], lhsT=wc[:, 2 * G + e, kg, :].bitcast(FP8X4),
+                                        lhsT_scale=ws[:, 2 * G + e, kg, :],
+                                        rhs=hc[:, kg, bs].bitcast(FP8X4), rhs_scale=hs[:, kg, bs],
+                                        start=(kg == 0), stop=(kg == 1))
+                gh[G] = ps
+            if e == 0:
+                pr[s // 2] = {"un": work.tile([P, 2, NB], F32, name="un", tag="un", bufs=4),
+                              "uz": work.tile([P, 2, NB], F32, name="uz", tag="uz", bufs=4)}
+            ut[s] = {"gi_r": gi_r, "gi_n": gi_n, "gi_z": gi_z, "gh": gh,
+                     "ar": work.tile([P, NB], F32, name="ar", tag="ar", bufs=2),
+                     "qn": work.tile([P, NB], F32, name="qn", tag="qn", bufs=3)}
+
+        def stt(dst, in0, scalar, in1, op0, op1):
+            nc.vector.scalar_tensor_tensor(out=dst, in0=in0, scalar=scalar, in1=in1, op0=op0, op1=op1)
+
+        def slot(s):
+            c, bh, e = unit_of(s)
+            k = s % 4
+            main = s < NSLOT
+            jobs = []
+            if main and k == 0 and c + 2 < 4:
+                load_w(c + 2)
+            if main and c + 1 < 4:
+                if k == 0:
+                    begin_w(c + 1)
+                if k < 3:
+                    jobs = [job_w(c + 1, 2 * k), job_w(c + 1, 2 * k + 1)]
+                else:
+                    jobs = [job_ia(c + 1), job_ib(c + 1)]
+            ojob = None
+            so = s - OLAG
+            if 0 <= so < NSLOT:
+                ojob = job_o(so // 4, so % 4)
+            ts = []
+            for j in jobs:
+                ts.extend(j[0])
+            if ojob is not None:
+                ts.extend(ojob[0])
+            if main:
+                pe_unit(s, ts)
+                u = ut[s]
+                pp = pr[s // 2]
+                w01 = wt[c]["w01"]
+                bs = slice(bh * NB, (bh + 1) * NB)
+                x0 = xb_v[:, bs, 0]
+                x1 = xb_v[:, bs, 1]
+                un = pp["un"][:, e, :]
+                uz = pp["uz"][:, e, :]
+                ar = u["ar"]
+                nc.scalar.copy(out=ar[:], in_=u["gi_r"][:])
+                if len(jobs) > 0:
+                    jobs[0][1]("act")
+                if e == 0:
+                    nc.scalar.copy(out=uz, in_=u["gi_z"][:])
+                if len(jobs) > 1:
+                    jobs[1][1]("act")
+                if c + 1 < 4 and 1 <= k:
+                    quant_w(c + 1, k - 1)
+                if c + 1 < 4 and k == 2:
+                    small_w(c + 1)
+                stt(un, x0, w01[:, 2, e, 0:1], u["gi_n"][:], ALU.mult, ALU.add)
+                if e == 1:
+                    stt(uz, x0, w01[:, 1, e, 0:1], u["gi_z"][:], ALU.mult, ALU.add)
+                nc.vector.tensor_tensor(out=ar[:], in0=u["gh"][0][:], in1=ar[:], op=ALU.add)
+                nc.scalar.activation(out=ar[:], in_=ar[:], func=AF.Sigmoid, bias=b_r[:, c, e:e + 1], scale=1.0)
+                if ojob is not None:
+                    ojob[1]("dve")
+                if e == 0:
+                    nc.vector.tensor_tensor(out=uz, in0=u["gh"][1][:], in1=uz, op=ALU.add)
+                else:
+                    pp["vz"] = work.tile([P, NB], F32, name="vz", tag="vz", bufs=2)
+                    stt(pp["vz"][:], x1, w01[:, 1, e, 1:2], u["gh"][1][:], ALU.mult, ALU.add)
+                stt(un, x1, w01[:, 2, e, 1:2], un, ALU.mult, ALU.add)
+                stt(u["qn"][:], u["gh"][2][:], b_hn[:, c, e:e + 1], ar[:], ALU.add, ALU.mult)
+            else:
+                for t in ts:
+                    t()
+                if ojob is not None:
+                    ojob[1]("dve")
+            if 1 <= s <= NSLOT:
+                c1, bh1, e1 = unit_of(s - 1)
+                p1 = pr[(s - 1) // 2]
+                nc.scalar.activation(out=p1["un"][:, e1, :], in_=p1["un"][:, e1, :], func=AF.Tanh,
+                                     bias=b_in[:, c1, e1:e1 + 1], scale=1.0)
+                nc.scalar.activation(out=p1["uz"][:, e1, :], in_=p1["uz"][:, e1, :], func=AF.Sigmoid,
+                                     bias=b_zn[:, c1, e1:e1 + 1], scale=-1.0)
+            if main:
+                nc.gpsimd.tensor_tensor(out=un, in0=un, in1=u["qn"][:], op=ALU.add)
+            if s % 2 == 1:
+                p = s // 2
+                if main:
+                    nc.gpsimd.tensor_tensor(out=pr[p]["uz"][:, 1, :], in0=pr[p]["uz"][:, 1, :],
+                                            in1=pr[p]["vz"][:], op=ALU.add)
+                if 0 <= p - 1 < NSLOT // 2:
+                    pair_f(p - 1)
+            else:
+                p = s // 2 - 1
+                if 0 <= p < NSLOT // 2:
+                    pair_d(p)
+
+        def pair_d(p):
+            c, bh = p // 2, p % 2
+            g, u2 = c // 2, c % 2
+            bs = slice(bh * NB, (bh + 1) * NB)
+            un = pr[p]["un"]
+            nc.gpsimd.tensor_tensor(out=un[:], in0=un[:],
+                                    in1=hg[:, g, bs, 2 * u2:2 * u2 + 2].rearrange("p b e -> p e b"),
+                                    op=ALU.subtract)
+
+        def pair_f(p):
+            c, bh = p // 2, p % 2
+            bs = slice(bh * NB, (bh + 1) * NB)
+            if bh == 0:
+                ft[c] = work.tile([P, 2, B], F32, name="f_t", tag="f_t", bufs=2)
+            nc.gpsimd.tensor_tensor(out=ft[c][:, :, bs], in0=pr[p]["uz"][:], in1=pr[p]["un"][:], op=ALU.mult)
+
+        for s in range(NSLOT + OLAG):
+            slot(s)

@@ -17,20 +17,30 @@ H = 1024
 IN = 258
 NB = 512
 NSLOT = 16
-OLAG = 6
+O_AT = {6: [(0, 0)], 7: [(0, 1)], 8: [(0, 2)], 9: [(0, 3)], 10: [(1, 0)], 11: [(1, 1)], 12: [(1, 2)], 13: [(1, 3)], 14: [(2, 0), (2, 1)], 15: [(2, 2), (2, 3)], 16: [(3, 0), (3, 1)], 17: [(3, 2), (3, 3)]}
+PD = 6
+LASTP = NSLOT // 2 - 1
 FLOPS = 2 * B * 3 * H * (H + IN)
 
 
-def weave(ms, ts):
+def weave(ms, ts, late):
     gaps = len(ms) - 1
-    k = 0
+    total = len(ts) + len(late)
+    first = list(ts)
+    second = list(late)
+    done = 0
     for i, m in enumerate(ms):
         m()
         if i < gaps:
-            hi = ((i + 1) * len(ts) + gaps - 1) // gaps
-            while k < hi:
-                ts[k]()
-                k += 1
+            hi = ((i + 1) * total + gaps - 1) // gaps
+            while done < hi:
+                if i >= 2 and len(second) > 0:
+                    second.pop(0)()
+                elif len(first) > 0:
+                    first.pop(0)()
+                else:
+                    break
+                done += 1
 
 
 def tile_wavernncell_pa_kernel(tc, x, feat, aux1, h, w_ih, w_hh, b_ih, b_hh, out):
@@ -79,6 +89,7 @@ def tile_wavernncell_pa_kernel(tc, x, feat, aux1, h, w_ih, w_hh, b_ih, b_hh, out
         ut = {}
         pr = {}
         ft = {}
+        ra = {}
 
         def load_w(c):
             win = wpool.tile([P, 3, 2 * IN], BF16, name="win", tag="win")
@@ -106,11 +117,13 @@ def tile_wavernncell_pa_kernel(tc, x, feat, aux1, h, w_ih, w_hh, b_ih, b_hh, out
         nc.scalar.activation(out=warm[:], in_=warm[:], func=AF.Sigmoid)
         win0 = wpool.tile([P, 3, 2 * IN], BF16, name="win", tag="win")
         nc.sync.dma_start(out=win0[:], in_=wih_v[0])
-        for k in range(4):
+        for k in range(2):
             nc.sync.dma_start(out=hn[:, 2 * k:2 * k + 2, :], in_=h_v[:, 2 * k:2 * k + 2, :])
         wn0 = wpool.tile([P, 3, 2 * H], BF16, name="wn", tag="wn")
         for G in range(3):
             nc.sync.dma_start(out=wn0[:, G, :], in_=whh_v[0, :, G, :])
+        for k in range(2, 4):
+            nc.sync.dma_start(out=hn[:, 2 * k:2 * k + 2, :], in_=h_v[:, 2 * k:2 * k + 2, :])
         wt[0] = {"win": win0, "wn": wn0}
         load_w(1)
 
@@ -148,9 +161,9 @@ def tile_wavernncell_pa_kernel(tc, x, feat, aux1, h, w_ih, w_hh, b_ih, b_hh, out
 
         def small_w(c):
             win_v = wt[c]["win"][:].rearrange("p G (e k) -> p G e k", e=2)
-            nc.vector.tensor_copy(out=wt[c]["w01"][:], in_=win_v[:, :, :, 256:258])
-            nc.vector.tensor_copy(out=wx[:, c, 0:2, 0:2], in_=win_v[:, 0, :, 256:258])
-            nc.vector.tensor_copy(out=wx[:, c, 2, 0:2], in_=win_v[:, 1, 0, 256:258])
+            nc.scalar.copy(out=wt[c]["w01"][:], in_=win_v[:, :, :, 256:258])
+            nc.scalar.copy(out=wx[:, c, 0:2, 0:2], in_=win_v[:, 0, :, 256:258])
+            nc.scalar.copy(out=wx[:, c, 2, 0:2], in_=win_v[:, 2, 0, 256:258])
 
         def job_ia(c):
             win_v = wt[c]["win"][:].rearrange("p G (e k) -> p G e k", e=2)
@@ -218,16 +231,13 @@ def tile_wavernncell_pa_kernel(tc, x, feat, aux1, h, w_ih, w_hh, b_ih, b_hh, out
         run_job(job_ia(0), "act")
         run_job(job_ib(0), "dve")
         run_job(job_rows(xn, x_t), "act")
-        for t in range(8):
+        for t in range(4):
             run_job(job_h(t), "act" if t % 2 == 0 else "dve")
-            if t == 4:
-                quant_h(0, 0)
-                quant_h(1, 0)
         for ge in range(6):
             run_job(job_w(0, ge), "act" if ge % 2 == 0 else "dve")
             if ge == 0:
-                quant_h(0, 1)
-                quant_h(1, 1)
+                quant_h(0, 0)
+                quant_h(1, 0)
             if ge == 3:
                 quant_w(0, 0)
             if ge == 5:
@@ -246,26 +256,45 @@ def tile_wavernncell_pa_kernel(tc, x, feat, aux1, h, w_ih, w_hh, b_ih, b_hh, out
         def mm(ps, lhsT, rhs, start, stop):
             return lambda: nc.tensor.matmul(ps[:], lhsT=lhsT, rhs=rhs, start=start, stop=stop)
 
+        def tacc(dst, src, stop):
+            return lambda: nc.tensor.matmul(dst, lhsT=src, rhs=ident_f[:], is_transpose=True, start=False, stop=stop)
+
+        def pe_ra(s):
+            c, bh, e = unit_of(s)
+            wc, ws = wt[c]["wc"], wt[c]["ws"]
+            ps = acc.tile([P, 4, P], F32, name="gra", tag="acc")
+            for i in range(4):
+                cs = slice(bh * NB + i * P, bh * NB + (i + 1) * P)
+                for kg in range(2):
+                    nc.tensor.matmul_mx(ps[:, i, :], lhsT=hc[:, kg, cs].bitcast(FP8X4), lhsT_scale=hs[:, kg, cs],
+                                        rhs=wc[:, e, kg, :].bitcast(FP8X4), rhs_scale=ws[:, e, kg, :],
+                                        start=(kg == 0), stop=(kg == 1))
+            ra[s] = work.tile([P, 4, P], F32, name="grs", tag="grs", bufs=2)
+            return lambda: nc.scalar.copy(out=ra[s][:], in_=ps[:])
+
         def pe_unit(s, ts):
             c, bh, e = unit_of(s)
             w = wt[c]
             wit, wc, ws = w["wit"], w["wc"], w["ws"]
             bs = slice(bh * NB, (bh + 1) * NB)
             gi_r = acc.tile([P, NB], F32, name="gi_r", tag="acc")
-            gi_n = acc.tile([P, NB], F32, name="gi_n", tag="acc")
             gi_z = acc.tile([P, NB], F32, name="gi_z", tag="acc")
+            gi_n = acc.tile([P, NB], F32, name="gi_n", tag="acc")
             ms = [mm(gi_r, wit[:, 2 * e, :], feat_t[:, bs], True, False),
                   mm(gi_r, wit[:, 2 * e + 1, :], aux_t[:, bs], False, False),
-                  mm(gi_r, wit[:, 12 + e, :], x_t[:, bs], False, True),
-                  mm(gi_n, wit[:, 8 + 2 * e, :], feat_t[:, bs], True, False),
-                  mm(gi_n, wit[:, 8 + 2 * e + 1, :], aux_t[:, bs], False, True),
+                  mm(gi_r, wit[:, 12 + e, :], x_t[:, bs], False, False),
                   mm(gi_z, wit[:, 4 + 2 * e, :], feat_t[:, bs], True, False),
-                  mm(gi_z, wit[:, 4 + 2 * e + 1, :], aux_t[:, bs], False, e == 1)]
+                  mm(gi_z, wit[:, 4 + 2 * e + 1, :], aux_t[:, bs], False, True),
+                  mm(gi_n, wit[:, 8 + 2 * e, :], feat_t[:, bs], True, False),
+                  mm(gi_n, wit[:, 8 + 2 * e + 1, :], aux_t[:, bs], False, e == 1)]
             if e == 0:
-                ms.append(mm(gi_z, wit[:, 14, :], x_t[:, bs], False, True))
-            weave(ms, ts)
+                ms.append(mm(gi_n, wit[:, 14, :], x_t[:, bs], False, True))
+            grs = ra[s]
+            late = [tacc(gi_r[:, i * P:(i + 1) * P], grs[:, i, :], i == 3) for i in range(4)]
+            weave(ms, ts, late)
+            ra_out = pe_ra(s + 1) if s + 1 < NSLOT else None
             gh = {}
-            for G in (0, 1, 2):
+            for G in (1, 2):
                 ps = acc.tile([P, NB], F32, name="gh%d" % G, tag="acc")
                 for kg in range(2):
                     nc.tensor.matmul_mx(ps[:], lhsT=wc[:, 2 * G + e, kg, :].bitcast(FP8X4),
@@ -275,114 +304,148 @@ def tile_wavernncell_pa_kernel(tc, x, feat, aux1, h, w_ih, w_hh, b_ih, b_hh, out
                 gh[G] = ps
             if e == 0:
                 pr[s // 2] = {"un": work.tile([P, 2, NB], F32, name="un", tag="un", bufs=4),
-                              "uz": work.tile([P, 2, NB], F32, name="uz", tag="uz", bufs=4)}
-            ut[s] = {"gi_r": gi_r, "gi_n": gi_n, "gi_z": gi_z, "gh": gh,
+                              "uz": work.tile([P, 2, NB], F32, name="uz", tag="uz", bufs=4),
+                              "vz": work.tile([P, 2, NB], F32, name="vz", tag="vz", bufs=2)}
+            ut[s] = {"ra_out": ra_out, "gi_r": gi_r, "gi_n": gi_n, "gi_z": gi_z, "gh": gh,
                      "ar": work.tile([P, NB], F32, name="ar", tag="ar", bufs=2),
                      "qn": work.tile([P, NB], F32, name="qn", tag="qn", bufs=3)}
 
         def stt(dst, in0, scalar, in1, op0, op1):
             nc.vector.scalar_tensor_tensor(out=dst, in0=in0, scalar=scalar, in1=in1, op0=op0, op1=op1)
 
+        def tt(eng, dst, in0, in1, op):
+            if eng == "dve":
+                nc.vector.tensor_tensor(out=dst, in0=in0, in1=in1, op=op)
+            else:
+                nc.gpsimd.tensor_tensor(out=dst, in0=in0, in1=in1, op=op)
+
+        def h_t(p, i):
+            c, bh = p // 2, p % 2
+            return hg[:, c // 2, bh * NB:(bh + 1) * NB, 2 * (c % 2) + i]
+
+        def sub_h(eng, p, lo, hi):
+            un = pr[p]["un"]
+            for i in range(lo, hi):
+                tt(eng, un[:, i, :], un[:, i, :], h_t(p, i), ALU.subtract)
+
+        def mul_z(eng, p, lo, hi):
+            c, bh = p // 2, p % 2
+            if c not in ft:
+                ft[c] = work.tile([P, 2, B], F32, name="f_t", tag="f_t", bufs=2)
+            for i in range(lo, hi):
+                tt(eng, ft[c][:, i, bh * NB:(bh + 1) * NB], pr[p]["uz"][:, i, :], pr[p]["un"][:, i, :], ALU.mult)
+
+        def prep_jobs(s):
+            c, k = s // 4 + 1, s % 4
+            if c > 3:
+                return []
+            seq = [("w", c, ge) for ge in range(6)] + [("ia", c, 0), ("ib", c, 0)]
+            cuts = (0, 0, 3, 6, 8) if c == 1 else (0, 2, 4, 6, 8)
+            return seq[cuts[k]:cuts[k + 1]]
+
+        def make_job(d):
+            if d[0] == "w":
+                if d[2] == 0:
+                    begin_w(d[1])
+                return job_w(d[1], d[2])
+            if d[0] == "ia":
+                return job_ia(d[1])
+            if d[0] == "ib":
+                return job_ib(d[1])
+            return job_o(d[1], d[2])
+
         def slot(s):
             c, bh, e = unit_of(s)
             k = s % 4
+            p = s // 2
             main = s < NSLOT
-            jobs = []
             if main and k == 0 and c + 2 < 4:
                 load_w(c + 2)
-            if main and c + 1 < 4:
-                if k == 0:
-                    begin_w(c + 1)
-                if k < 3:
-                    jobs = [job_w(c + 1, 2 * k), job_w(c + 1, 2 * k + 1)]
-                else:
-                    jobs = [job_ia(c + 1), job_ib(c + 1)]
-            ojob = None
-            so = s - OLAG
-            if 0 <= so < NSLOT:
-                ojob = job_o(so // 4, so % 4)
+            jobs = [make_job(d) for d in prep_jobs(s)] if main else []
+            ojobs = [job_o(co, io) for co, io in O_AT.get(s, [])]
             ts = []
-            for j in jobs:
+            for j in jobs + ojobs:
                 ts.extend(j[0])
-            if ojob is not None:
-                ts.extend(ojob[0])
             if main:
                 pe_unit(s, ts)
                 u = ut[s]
-                pp = pr[s // 2]
+                pp = pr[p]
                 w01 = wt[c]["w01"]
                 bs = slice(bh * NB, (bh + 1) * NB)
                 x0 = xb_v[:, bs, 0]
                 x1 = xb_v[:, bs, 1]
                 un = pp["un"][:, e, :]
                 uz = pp["uz"][:, e, :]
+                vz = pp["vz"][:, e, :]
                 ar = u["ar"]
-                nc.scalar.copy(out=ar[:], in_=u["gi_r"][:])
-                if len(jobs) > 0:
-                    jobs[0][1]("act")
-                if e == 0:
-                    nc.scalar.copy(out=uz, in_=u["gi_z"][:])
-                if len(jobs) > 1:
-                    jobs[1][1]("act")
-                if c + 1 < 4 and 1 <= k:
-                    quant_w(c + 1, k - 1)
+                nc.scalar.activation(out=ar[:], in_=u["gi_r"][:], func=AF.Sigmoid, bias=b_r[:, c, e:e + 1], scale=1.0)
+                for j in jobs:
+                    j[1]("act")
+                if u["ra_out"] is not None:
+                    u["ra_out"]()
                 if c + 1 < 4 and k == 2:
                     small_w(c + 1)
-                stt(un, x0, w01[:, 2, e, 0:1], u["gi_n"][:], ALU.mult, ALU.add)
+                for d in prep_jobs(s - 1) if s > 0 else []:
+                    if d[0] == "w" and d[2] % 2 == 1:
+                        quant_w(d[1], d[2] // 2)
+                stt(uz, x0, w01[:, 1, e, 0:1], u["gi_z"][:], ALU.mult, ALU.add)
                 if e == 1:
-                    stt(uz, x0, w01[:, 1, e, 0:1], u["gi_z"][:], ALU.mult, ALU.add)
-                nc.vector.tensor_tensor(out=ar[:], in0=u["gh"][0][:], in1=ar[:], op=ALU.add)
-                nc.scalar.activation(out=ar[:], in_=ar[:], func=AF.Sigmoid, bias=b_r[:, c, e:e + 1], scale=1.0)
-                if ojob is not None:
-                    ojob[1]("dve")
-                if e == 0:
-                    nc.vector.tensor_tensor(out=uz, in0=u["gh"][1][:], in1=uz, op=ALU.add)
-                else:
-                    pp["vz"] = work.tile([P, NB], F32, name="vz", tag="vz", bufs=2)
-                    stt(pp["vz"][:], x1, w01[:, 1, e, 1:2], u["gh"][1][:], ALU.mult, ALU.add)
-                stt(un, x1, w01[:, 2, e, 1:2], un, ALU.mult, ALU.add)
+                    stt(un, x0, w01[:, 2, e, 0:1], u["gi_n"][:], ALU.mult, ALU.add)
+                for j in ojobs:
+                    j[1]("dve")
+                stt(vz, x1, w01[:, 1, e, 1:2], u["gh"][1][:], ALU.mult, ALU.add)
+                if e == 1:
+                    stt(un, x1, w01[:, 2, e, 1:2], un, ALU.mult, ALU.add)
                 stt(u["qn"][:], u["gh"][2][:], b_hn[:, c, e:e + 1], ar[:], ALU.add, ALU.mult)
+                if e == 0:
+                    tt("dve", un, u["gi_n"][:], u["qn"][:], ALU.add)
+                if p >= PD:
+                    if e == 1:
+                        tt("dve", un, un, u["qn"][:], ALU.add)
+                    tt("dve", uz, uz, vz, ALU.add)
             else:
                 for t in ts:
                     t()
-                if ojob is not None:
-                    ojob[1]("dve")
+                for j in ojobs:
+                    j[1]("dve")
             if 1 <= s <= NSLOT:
-                c1, bh1, e1 = unit_of(s - 1)
-                p1 = pr[(s - 1) // 2]
-                nc.scalar.activation(out=p1["un"][:, e1, :], in_=p1["un"][:, e1, :], func=AF.Tanh,
-                                     bias=b_in[:, c1, e1:e1 + 1], scale=1.0)
-                nc.scalar.activation(out=p1["uz"][:, e1, :], in_=p1["uz"][:, e1, :], func=AF.Sigmoid,
-                                     bias=b_zn[:, c1, e1:e1 + 1], scale=-1.0)
-            if main:
-                nc.gpsimd.tensor_tensor(out=un, in0=un, in1=u["qn"][:], op=ALU.add)
-            if s % 2 == 1:
-                p = s // 2
-                if main:
-                    nc.gpsimd.tensor_tensor(out=pr[p]["uz"][:, 1, :], in0=pr[p]["uz"][:, 1, :],
-                                            in1=pr[p]["vz"][:], op=ALU.add)
-                if 0 <= p - 1 < NSLOT // 2:
-                    pair_f(p - 1)
-            else:
-                p = s // 2 - 1
-                if 0 <= p < NSLOT // 2:
-                    pair_d(p)
+                tanh_of(s - 1)
+                if (s - 1) // 2 >= PD:
+                    sig_z(s - 1)
+                elif s % 2 == 0:
+                    sig_z(s - 2)
+                    sig_z(s - 1)
+            if main and s % 2 == 1 and p < PD:
+                tt("pool", un, un, u["qn"][:], ALU.add)
+                tt("pool", pp["uz"][:], pp["uz"][:], pp["vz"][:], ALU.add)
+            if s % 2 == 1 and 1 <= p <= PD:
+                mul_z("pool", p - 1, 0, 2)
+            if s % 2 == 0 and 1 <= p <= LASTP:
+                sub_h("pool", p - 1, 0, 2)
+                if p - 1 >= PD:
+                    mul_z("pool", p - 1, 0, 2)
+            if s == NSLOT - 1:
+                sub_h("pool", LASTP, 0, 1)
+                mul_z("pool", LASTP, 0, 1)
+            if s == NSLOT:
+                sub_h("dve", LASTP, 1, 2)
+                mul_z("dve", LASTP, 1, 2)
 
-        def pair_d(p):
-            c, bh = p // 2, p % 2
-            g, u2 = c // 2, c % 2
-            bs = slice(bh * NB, (bh + 1) * NB)
-            un = pr[p]["un"]
-            nc.gpsimd.tensor_tensor(out=un[:], in0=un[:],
-                                    in1=hg[:, g, bs, 2 * u2:2 * u2 + 2].rearrange("p b e -> p e b"),
-                                    op=ALU.subtract)
+        def tanh_of(s):
+            c1, bh1, e1 = unit_of(s)
+            un1 = pr[s // 2]["un"][:, e1, :]
+            nc.scalar.activation(out=un1, in_=un1, func=AF.Tanh, bias=b_in[:, c1, e1:e1 + 1], scale=1.0)
 
-        def pair_f(p):
-            c, bh = p // 2, p % 2
-            bs = slice(bh * NB, (bh + 1) * NB)
-            if bh == 0:
-                ft[c] = work.tile([P, 2, B], F32, name="f_t", tag="f_t", bufs=2)
-            nc.gpsimd.tensor_tensor(out=ft[c][:, :, bs], in0=pr[p]["uz"][:], in1=pr[p]["un"][:], op=ALU.mult)
+        def sig_z(s):
+            c1, bh1, e1 = unit_of(s)
+            uz1 = pr[s // 2]["uz"][:, e1, :]
+            nc.scalar.activation(out=uz1, in_=uz1, func=AF.Sigmoid, bias=b_zn[:, c1, e1:e1 + 1], scale=-1.0)
 
-        for s in range(NSLOT + OLAG):
+        pe_ra(0)()
+        for s in range(NSLOT + 2):
             slot(s)
+            if s == 0:
+                for t in range(4, 8):
+                    run_job(job_h(t), "act" if t % 2 == 0 else "dve")
+                quant_h(0, 1)
+                quant_h(1, 1)

@@ -18,7 +18,7 @@ IN = 258
 NB = 512
 NSLOT = 16
 O_AT = {6: [(0, 0)], 7: [(0, 1)], 8: [(0, 2)], 9: [(0, 3)], 10: [(1, 0)], 11: [(1, 1)], 12: [(1, 2)], 13: [(1, 3)], 14: [(2, 0), (2, 1)], 15: [(2, 2), (2, 3)], 16: [(3, 0), (3, 1)], 17: [(3, 2), (3, 3)]}
-PD = 6
+PD = 0
 LASTP = NSLOT // 2 - 1
 FLOPS = 2 * B * 3 * H * (H + IN)
 
@@ -90,6 +90,7 @@ def tile_wavernncell_pa_kernel(tc, x, feat, aux1, h, w_ih, w_hh, b_ih, b_hh, out
         pr = {}
         ft = {}
         ra = {}
+        nt = {}
 
         def load_w(c):
             win = wpool.tile([P, 3, 2 * IN], BF16, name="win", tag="win")
@@ -155,7 +156,7 @@ def tile_wavernncell_pa_kernel(tc, x, feat, aux1, h, w_ih, w_hh, b_ih, b_hh, out
             w = wt[c]
             w["w01"] = wpool.tile([P, 3, 2, 2], F32, name="w01", tag="w01")
             w["wit"] = wpool.tile([P, 15, P], BF16, name="wit", tag="wit")
-            w["wg"] = wpool.tile([P, 6, 2, P, 4], BF16, name="wg", tag="wg", align_bytes=64)
+            w["wg"] = wpool.tile([P, 6, 2, P, 4], BF16, name="wg", tag="wg", bufs=1, align_bytes=64)
             w["wc"] = wpool.tile([P, 6, 2, P], U32, name="wc", tag="wc", align_bytes=64)
             w["ws"] = wpool.tile([P, 6, 2, P], U8, name="ws", tag="ws", align_bytes=64)
 
@@ -203,19 +204,25 @@ def tile_wavernncell_pa_kernel(tc, x, feat, aux1, h, w_ih, w_hh, b_ih, b_hh, out
             nc.vector.quantize_mx(out=hc[:, g, bs].bitcast(FP8X4), scales=hs[:, g, bs],
                                   in_=hg[:, g, bs, :].rearrange("p b t -> p (b t)"))
 
+        def tsum(dst, src, start, stop):
+            return lambda: nc.tensor.matmul(dst, lhsT=src, rhs=ident_f[:], is_transpose=True, start=start, stop=stop)
+
         def job_o(c, i):
             f_t = ft[c]
             js = slice(256 * c, 256 * (c + 1))
             pt = tp.tile([P, 2, 2, P], F32, name="pt_o", tag="tp")
-            ts = [tr(pt[:, k, e, :], f_t[:, e, (2 * i + k) * P:(2 * i + k + 1) * P], ident_f)
-                  for k in range(2) for e in range(2)]
+            n_t = nt[c]
+            ts = []
+            for k in range(2):
+                for e in range(2):
+                    cs = slice((2 * i + k) * P, (2 * i + k + 1) * P)
+                    ts.append(tsum(pt[:, k, e, :], n_t[:, e, cs], True, False))
+                    ts.append(tsum(pt[:, k, e, :], f_t[:, e, cs], False, True))
 
             def ev(eng):
                 o_t = work.tile([P, 2, 256], F32, name="o_t", tag="o_t", bufs=3)
-                nc.vector.tensor_tensor(out=o_t[:].rearrange("p k (q e) -> p k q e", e=2),
-                                        in0=pt[:].rearrange("p k e q -> p k q e"),
-                                        in1=hn[:, 2 * i:2 * i + 2, js].rearrange("p k (q e) -> p k q e", e=2),
-                                        op=ALU.add)
+                nc.scalar.copy(out=o_t[:].rearrange("p k (q e) -> p k q e", e=2),
+                               in_=pt[:].rearrange("p k e q -> p k q e"))
                 nc.sync.dma_start(out=out_v[:, 2 * i:2 * i + 2, js], in_=o_t[:])
             return ts, ev
 
@@ -244,8 +251,7 @@ def tile_wavernncell_pa_kernel(tc, x, feat, aux1, h, w_ih, w_hh, b_ih, b_hh, out
                 quant_w(0, 1)
         quant_w(0, 2)
         nc.vector.tensor_tensor(out=b_r[:], in0=bi[:, 0:4, :], in1=bh2[:, 0:4, :], op=ALU.add)
-        nc.vector.scalar_tensor_tensor(out=b_zn[:], in0=bi[:, 4:8, :], scalar=-1.0, in1=bh2[:, 4:8, :],
-                                       op0=ALU.mult, op1=ALU.subtract)
+        nc.vector.tensor_tensor(out=b_zn[:], in0=bi[:, 4:8, :], in1=bh2[:, 4:8, :], op=ALU.add)
         nc.vector.tensor_copy(out=b_in[:], in_=bi[:, 8:12, :])
         nc.vector.tensor_copy(out=b_hn[:], in_=bh2[:, 8:12, :])
 
@@ -292,9 +298,8 @@ def tile_wavernncell_pa_kernel(tc, x, feat, aux1, h, w_ih, w_hh, b_ih, b_hh, out
             grs = ra[s]
             late = [tacc(gi_r[:, i * P:(i + 1) * P], grs[:, i, :], i == 3) for i in range(4)]
             weave(ms, ts, late)
-            ra_out = pe_ra(s + 1) if s + 1 < NSLOT else None
             gh = {}
-            for G in (1, 2):
+            for G in (2, 1):
                 ps = acc.tile([P, NB], F32, name="gh%d" % G, tag="acc")
                 for kg in range(2):
                     nc.tensor.matmul_mx(ps[:], lhsT=wc[:, 2 * G + e, kg, :].bitcast(FP8X4),
@@ -302,9 +307,10 @@ def tile_wavernncell_pa_kernel(tc, x, feat, aux1, h, w_ih, w_hh, b_ih, b_hh, out
                                         rhs=hc[:, kg, bs].bitcast(FP8X4), rhs_scale=hs[:, kg, bs],
                                         start=(kg == 0), stop=(kg == 1))
                 gh[G] = ps
+            ra_out = pe_ra(s + 1) if s + 1 < NSLOT else None
             if e == 0:
-                pr[s // 2] = {"un": work.tile([P, 2, NB], F32, name="un", tag="un", bufs=4),
-                              "uz": work.tile([P, 2, NB], F32, name="uz", tag="uz", bufs=4),
+                pr[s // 2] = {"un": work.tile([P, 2, NB], F32, name="un", tag="un", bufs=3),
+                              "uz": work.tile([P, 2, NB], F32, name="uz", tag="uz", bufs=3),
                               "vz": work.tile([P, 2, NB], F32, name="vz", tag="vz", bufs=2)}
             ut[s] = {"ra_out": ra_out, "gi_r": gi_r, "gi_n": gi_n, "gi_z": gi_z, "gh": gh,
                      "ar": work.tile([P, NB], F32, name="ar", tag="ar", bufs=2),
@@ -326,7 +332,7 @@ def tile_wavernncell_pa_kernel(tc, x, feat, aux1, h, w_ih, w_hh, b_ih, b_hh, out
         def sub_h(eng, p, lo, hi):
             un = pr[p]["un"]
             for i in range(lo, hi):
-                tt(eng, un[:, i, :], un[:, i, :], h_t(p, i), ALU.subtract)
+                tt(eng, un[:, i, :], h_t(p, i), nt[p // 2][:, i, (p % 2) * NB:(p % 2 + 1) * NB], ALU.subtract)
 
         def mul_z(eng, p, lo, hi):
             c, bh = p // 2, p % 2
@@ -391,14 +397,14 @@ def tile_wavernncell_pa_kernel(tc, x, feat, aux1, h, w_ih, w_hh, b_ih, b_hh, out
                 stt(uz, x0, w01[:, 1, e, 0:1], u["gi_z"][:], ALU.mult, ALU.add)
                 if e == 1:
                     stt(un, x0, w01[:, 2, e, 0:1], u["gi_n"][:], ALU.mult, ALU.add)
-                for j in ojobs:
-                    j[1]("dve")
-                stt(vz, x1, w01[:, 1, e, 1:2], u["gh"][1][:], ALU.mult, ALU.add)
                 if e == 1:
                     stt(un, x1, w01[:, 2, e, 1:2], un, ALU.mult, ALU.add)
                 stt(u["qn"][:], u["gh"][2][:], b_hn[:, c, e:e + 1], ar[:], ALU.add, ALU.mult)
                 if e == 0:
                     tt("dve", un, u["gi_n"][:], u["qn"][:], ALU.add)
+                stt(vz, x1, w01[:, 1, e, 1:2], u["gh"][1][:], ALU.mult, ALU.add)
+                for j in ojobs:
+                    j[1]("dve")
                 if p >= PD:
                     if e == 1:
                         tt("dve", un, un, u["qn"][:], ALU.add)
@@ -434,12 +440,15 @@ def tile_wavernncell_pa_kernel(tc, x, feat, aux1, h, w_ih, w_hh, b_ih, b_hh, out
         def tanh_of(s):
             c1, bh1, e1 = unit_of(s)
             un1 = pr[s // 2]["un"][:, e1, :]
-            nc.scalar.activation(out=un1, in_=un1, func=AF.Tanh, bias=b_in[:, c1, e1:e1 + 1], scale=1.0)
+            if c1 not in nt:
+                nt[c1] = work.tile([P, 2, B], F32, name="n_t", tag="n_t", bufs=2)
+            nc.scalar.activation(out=nt[c1][:, e1, bh1 * NB:(bh1 + 1) * NB], in_=un1, func=AF.Tanh,
+                                 bias=b_in[:, c1, e1:e1 + 1], scale=1.0)
 
         def sig_z(s):
             c1, bh1, e1 = unit_of(s)
             uz1 = pr[s // 2]["uz"][:, e1, :]
-            nc.scalar.activation(out=uz1, in_=uz1, func=AF.Sigmoid, bias=b_zn[:, c1, e1:e1 + 1], scale=-1.0)
+            nc.scalar.activation(out=uz1, in_=uz1, func=AF.Sigmoid, bias=b_zn[:, c1, e1:e1 + 1], scale=1.0)
 
         pe_ra(0)()
         for s in range(NSLOT + 2):

@@ -24,23 +24,12 @@ FLOPS = 2 * B * 3 * H * (H + IN)
 
 
 def weave(ms, ts, late):
-    gaps = len(ms) - 1
-    total = len(ts) + len(late)
-    first = list(ts)
-    second = list(late)
-    done = 0
-    for i, m in enumerate(ms):
+    for m in ms[:3]:
         m()
-        if i < gaps:
-            hi = ((i + 1) * total + gaps - 1) // gaps
-            while done < hi:
-                if i >= 2 and len(second) > 0:
-                    second.pop(0)()
-                elif len(first) > 0:
-                    first.pop(0)()
-                else:
-                    break
-                done += 1
+    for t in late + ts:
+        t()
+    for m in ms[3:]:
+        m()
 
 
 def tile_wavernncell_pa_kernel(tc, x, feat, aux1, h, w_ih, w_hh, b_ih, b_hh, out):

@@ -18,18 +18,29 @@ IN = 258
 NB = 512
 NSLOT = 16
 O_AT = {6: [(0, 0)], 7: [(0, 1)], 8: [(0, 2)], 9: [(0, 3)], 10: [(1, 0)], 11: [(1, 1)], 12: [(1, 2)], 13: [(1, 3)], 14: [(2, 0), (2, 1)], 15: [(2, 2), (2, 3)], 16: [(3, 0), (3, 1)], 17: [(3, 2), (3, 3)]}
-PD = 0
+PD = 2
 LASTP = NSLOT // 2 - 1
 FLOPS = 2 * B * 3 * H * (H + IN)
 
 
 def weave(ms, ts, late):
-    for m in ms[:3]:
+    gaps = len(ms) - 1
+    total = len(ts) + len(late)
+    first = list(ts)
+    second = list(late)
+    done = 0
+    for i, m in enumerate(ms):
         m()
-    for t in late + ts:
-        t()
-    for m in ms[3:]:
-        m()
+        if i < gaps:
+            hi = ((i + 1) * total + gaps - 1) // gaps
+            while done < hi:
+                if i >= 3 and len(second) > 0:
+                    second.pop(0)()
+                elif len(first) > 0:
+                    first.pop(0)()
+                else:
+                    break
+                done += 1
 
 
 def tile_wavernncell_pa_kernel(tc, x, feat, aux1, h, w_ih, w_hh, b_ih, b_hh, out):
@@ -79,7 +90,6 @@ def tile_wavernncell_pa_kernel(tc, x, feat, aux1, h, w_ih, w_hh, b_ih, b_hh, out
         pr = {}
         ft = {}
         ra = {}
-        nt = {}
 
         def load_w(c):
             win = wpool.tile([P, 3, 2 * IN], BF16, name="win", tag="win")
@@ -145,7 +155,7 @@ def tile_wavernncell_pa_kernel(tc, x, feat, aux1, h, w_ih, w_hh, b_ih, b_hh, out
             w = wt[c]
             w["w01"] = wpool.tile([P, 3, 2, 2], F32, name="w01", tag="w01")
             w["wit"] = wpool.tile([P, 15, P], BF16, name="wit", tag="wit")
-            w["wg"] = wpool.tile([P, 6, 2, P, 4], BF16, name="wg", tag="wg", bufs=1, align_bytes=64)
+            w["wg"] = wpool.tile([P, 6, 2, P, 4], BF16, name="wg", tag="wg", align_bytes=64)
             w["wc"] = wpool.tile([P, 6, 2, P], U32, name="wc", tag="wc", align_bytes=64)
             w["ws"] = wpool.tile([P, 6, 2, P], U8, name="ws", tag="ws", align_bytes=64)
 
@@ -193,25 +203,19 @@ def tile_wavernncell_pa_kernel(tc, x, feat, aux1, h, w_ih, w_hh, b_ih, b_hh, out
             nc.vector.quantize_mx(out=hc[:, g, bs].bitcast(FP8X4), scales=hs[:, g, bs],
                                   in_=hg[:, g, bs, :].rearrange("p b t -> p (b t)"))
 
-        def tsum(dst, src, start, stop):
-            return lambda: nc.tensor.matmul(dst, lhsT=src, rhs=ident_f[:], is_transpose=True, start=start, stop=stop)
-
         def job_o(c, i):
             f_t = ft[c]
             js = slice(256 * c, 256 * (c + 1))
             pt = tp.tile([P, 2, 2, P], F32, name="pt_o", tag="tp")
-            n_t = nt[c]
-            ts = []
-            for k in range(2):
-                for e in range(2):
-                    cs = slice((2 * i + k) * P, (2 * i + k + 1) * P)
-                    ts.append(tsum(pt[:, k, e, :], n_t[:, e, cs], True, False))
-                    ts.append(tsum(pt[:, k, e, :], f_t[:, e, cs], False, True))
+            ts = [tr(pt[:, k, e, :], f_t[:, e, (2 * i + k) * P:(2 * i + k + 1) * P], ident_f)
+                  for k in range(2) for e in range(2)]
 
             def ev(eng):
                 o_t = work.tile([P, 2, 256], F32, name="o_t", tag="o_t", bufs=3)
-                nc.scalar.copy(out=o_t[:].rearrange("p k (q e) -> p k q e", e=2),
-                               in_=pt[:].rearrange("p k e q -> p k q e"))
+                nc.vector.tensor_tensor(out=o_t[:].rearrange("p k (q e) -> p k q e", e=2),
+                                        in0=pt[:].rearrange("p k e q -> p k q e"),
+                                        in1=hn[:, 2 * i:2 * i + 2, js].rearrange("p k (q e) -> p k q e", e=2),
+                                        op=ALU.add)
                 nc.sync.dma_start(out=out_v[:, 2 * i:2 * i + 2, js], in_=o_t[:])
             return ts, ev
 
@@ -240,7 +244,8 @@ def tile_wavernncell_pa_kernel(tc, x, feat, aux1, h, w_ih, w_hh, b_ih, b_hh, out
                 quant_w(0, 1)
         quant_w(0, 2)
         nc.vector.tensor_tensor(out=b_r[:], in0=bi[:, 0:4, :], in1=bh2[:, 0:4, :], op=ALU.add)
-        nc.vector.tensor_tensor(out=b_zn[:], in0=bi[:, 4:8, :], in1=bh2[:, 4:8, :], op=ALU.add)
+        nc.vector.scalar_tensor_tensor(out=b_zn[:], in0=bi[:, 4:8, :], scalar=-1.0, in1=bh2[:, 4:8, :],
+                                       op0=ALU.mult, op1=ALU.subtract)
         nc.vector.tensor_copy(out=b_in[:], in_=bi[:, 8:12, :])
         nc.vector.tensor_copy(out=b_hn[:], in_=bh2[:, 8:12, :])
 
@@ -298,8 +303,8 @@ def tile_wavernncell_pa_kernel(tc, x, feat, aux1, h, w_ih, w_hh, b_ih, b_hh, out
                 gh[G] = ps
             ra_out = pe_ra(s + 1) if s + 1 < NSLOT else None
             if e == 0:
-                pr[s // 2] = {"un": work.tile([P, 2, NB], F32, name="un", tag="un", bufs=3),
-                              "uz": work.tile([P, 2, NB], F32, name="uz", tag="uz", bufs=3),
+                pr[s // 2] = {"un": work.tile([P, 2, NB], F32, name="un", tag="un", bufs=4),
+                              "uz": work.tile([P, 2, NB], F32, name="uz", tag="uz", bufs=4),
                               "vz": work.tile([P, 2, NB], F32, name="vz", tag="vz", bufs=2)}
             ut[s] = {"ra_out": ra_out, "gi_r": gi_r, "gi_n": gi_n, "gi_z": gi_z, "gh": gh,
                      "ar": work.tile([P, NB], F32, name="ar", tag="ar", bufs=2),
@@ -321,7 +326,7 @@ def tile_wavernncell_pa_kernel(tc, x, feat, aux1, h, w_ih, w_hh, b_ih, b_hh, out
         def sub_h(eng, p, lo, hi):
             un = pr[p]["un"]
             for i in range(lo, hi):
-                tt(eng, un[:, i, :], h_t(p, i), nt[p // 2][:, i, (p % 2) * NB:(p % 2 + 1) * NB], ALU.subtract)
+                tt(eng, un[:, i, :], un[:, i, :], h_t(p, i), ALU.subtract)
 
         def mul_z(eng, p, lo, hi):
             c, bh = p // 2, p % 2
@@ -429,15 +434,12 @@ def tile_wavernncell_pa_kernel(tc, x, feat, aux1, h, w_ih, w_hh, b_ih, b_hh, out
         def tanh_of(s):
             c1, bh1, e1 = unit_of(s)
             un1 = pr[s // 2]["un"][:, e1, :]
-            if c1 not in nt:
-                nt[c1] = work.tile([P, 2, B], F32, name="n_t", tag="n_t", bufs=2)
-            nc.scalar.activation(out=nt[c1][:, e1, bh1 * NB:(bh1 + 1) * NB], in_=un1, func=AF.Tanh,
-                                 bias=b_in[:, c1, e1:e1 + 1], scale=1.0)
+            nc.scalar.activation(out=un1, in_=un1, func=AF.Tanh, bias=b_in[:, c1, e1:e1 + 1], scale=1.0)
 
         def sig_z(s):
             c1, bh1, e1 = unit_of(s)
             uz1 = pr[s // 2]["uz"][:, e1, :]
-            nc.scalar.activation(out=uz1, in_=uz1, func=AF.Sigmoid, bias=b_zn[:, c1, e1:e1 + 1], scale=1.0)
+            nc.scalar.activation(out=uz1, in_=uz1, func=AF.Sigmoid, bias=b_zn[:, c1, e1:e1 + 1], scale=-1.0)
 
         pe_ra(0)()
         for s in range(NSLOT + 2):

from contextlib import ExitStack

import concourse.mybir as mybir
from concourse.masks import make_identity

F32 = mybir.dt.float32
BF16 = mybir.dt.bfloat16
U32 = mybir.dt.uint32
U8 = mybir.dt.uint8
FP8X4 = mybir.dt.float8_e4m3fn_x4
ALU = mybir.AluOpType
AF = mybir.ActivationFunctionType

P = 128
B = 1024
H = 1024
IN = 258
NB = 512
NSLOT = 16
O_AT = {6: [(0, 0)], 7: [(0, 1)], 8: [(0, 2)], 9: [(0, 3)], 10: [(1, 0)], 11: [(1, 1)], 12: [(1, 2)], 13: [(1, 3)], 14: [(2, 0), (2, 1)], 15: [(2, 2), (2, 3)], 16: [(3, 0), (3, 1)], 17: [(3, 2), (3, 3)]}
PD = 2
LASTP = NSLOT // 2 - 1
FLOPS = 2 * B * 3 * H * (H + IN)


def weave(ms, ts, late):
    gaps = len(ms) - 1
    total = len(ts) + len(late)
    first = list(ts)
    second = list(late)
    done = 0
    for i, m in enumerate(ms):
        m()
        if i < gaps:
            hi = ((i + 1) * total + gaps - 1) // gaps
            while done < hi:
                if i >= 3 and len(second) > 0:
                    second.pop(0)()
                elif len(first) > 0:
                    first.pop(0)()
                else:
                    break
                done += 1


def tile_wavernncell_pa_kernel(tc, x, feat, aux1, h, w_ih, w_hh, b_ih, b_hh, out):
    nc = tc.nc
    with ExitStack() as ctx:
        ctx.enter_context(tc.manual_schedule())
        const = ctx.enter_context(tc.tile_pool(name="const", bufs=1))
        wpool = ctx.enter_context(tc.tile_pool(name="wpool", bufs=2))
        work = ctx.enter_context(tc.tile_pool(name="work", bufs=2))
        acc = ctx.enter_context(tc.psum_pool(name="acc", bufs=5))
        tp = ctx.enter_context(tc.psum_pool(name="tp", bufs=3))

        feat_v = feat.rearrange("(t p) k -> p t k", p=P)
        aux_v = aux1.rearrange("(t p) k -> p t k", p=P)
        x_v = x.rearrange("(t p) c -> p t c", p=P)
        h_v = h.rearrange("(t p) k -> p t k", p=P)
        out_v = out.rearrange("(t p) j -> p t j", p=P)
        wih_v = w_ih.rearrange("(G c q e) k -> c q G (e k)", G=3, c=4, q=P, e=2)
        whh_v = w_hh.rearrange("(G c q e) k -> c q G (e k)", G=3, c=4, q=P, e=2)
        bih_v = b_ih.rearrange("(m q e) -> q m e", m=12, q=P, e=2)
        bhh_v = b_hh.rearrange("(m q e) -> q m e", m=12, q=P, e=2)

        ident_f = const.tile([P, P], F32, name="ident_f")
        ident_b = const.tile([P, P], BF16, name="ident_b")
        warm = const.tile([P, 1], F32, name="warm")
        fn = const.tile([P, 8, P], BF16, name="fn")
        an = const.tile([P, 8, P], BF16, name="an")
        xn = const.tile([P, 8, P], BF16, name="xn")
        feat_t = const.tile([P, B], BF16, name="feat_t")
        aux_t = const.tile([P, B], BF16, name="aux_t")
        x_t = const.tile([P, B], BF16, name="x_t")
        xb = const.tile([P, 2 * B], BF16, name="xb")
        hn = const.tile([P, 8, H], BF16, name="hn")
        hg = const.tile([P, 2, B, 4], BF16, name="hg", align_bytes=64)
        hc = const.tile([P, 2, B], U32, name="hc", align_bytes=64)
        hs = const.tile([P, 2, B], U8, name="hs", align_bytes=64)
        wx = const.tile([P, 4, 3, P], BF16, name="wx")
        bi = const.tile([P, 12, 2], BF16, name="bi")
        bh2 = const.tile([P, 12, 2], BF16, name="bh2")
        b_r = const.tile([P, 4, 2], F32, name="b_r")
        b_zn = const.tile([P, 4, 2], F32, name="b_zn")
        b_in = const.tile([P, 4, 2], F32, name="b_in")
        b_hn = const.tile([P, 4, 2], F32, name="b_hn")

        wt = {}
        ut = {}
        pr = {}
        ft = {}
        ra = {}

        def load_w(c):
            win = wpool.tile([P, 3, 2 * IN], BF16, name="win", tag="win")
            wn = wpool.tile([P, 3, 2 * H], BF16, name="wn", tag="wn")
            if c == 0:
                nc.sync.dma_start(out=win[:], in_=wih_v[c])
            for G in range(3):
                nc.sync.dma_start(out=wn[:, G, :], in_=whh_v[c, :, G, :])
            if c > 0:
                nc.sync.dma_start(out=win[:], in_=wih_v[c])
            wt[c] = {"win": win, "wn": wn}

        nc.vector.memset(warm[:], 0.0)
        nc.vector.memset(xn[:], 0.0)
        nc.vector.memset(wx[:], 0.0)
        make_identity(nc, ident_b[:])
        make_identity(nc, ident_f[:])
        nc.sync.dma_start(out=fn[:], in_=feat_v)
        nc.sync.dma_start(out=an[:], in_=aux_v)
        with nc.allow_non_contiguous_dma(reason="small vectors, four bytes a piece"):
            nc.scalar.dma_start(out=xn[:, :, 0:2], in_=x_v)
            nc.scalar.dma_start(out=bi[:], in_=bih_v)
            nc.scalar.dma_start(out=bh2[:], in_=bhh_v)
        nc.scalar.dma_start(out=xb[:], in_=x.rearrange("b c -> (b c)").partition_broadcast(P))
        nc.scalar.activation(out=warm[:], in_=warm[:], func=AF.Sigmoid)
        win0 = wpool.tile([P, 3, 2 * IN], BF16, name="win", tag="win")
        nc.sync.dma_start(out=win0[:], in_=wih_v[0])
        for k in range(2):
            nc.sync.dma_start(out=hn[:, 2 * k:2 * k + 2, :], in_=h_v[:, 2 * k:2 * k + 2, :])
        wn0 = wpool.tile([P, 3, 2 * H], BF16, name="wn", tag="wn")
        for G in range(3):
            nc.sync.dma_start(out=wn0[:, G, :], in_=whh_v[0, :, G, :])
        for k in range(2, 4):
            nc.sync.dma_start(out=hn[:, 2 * k:2 * k + 2, :], in_=h_v[:, 2 * k:2 * k + 2, :])
        wt[0] = {"win": win0, "wn": wn0}
        load_w(1)

        xb_v = xb[:].rearrange("p (b c) -> p b c", c=2)
        hn_w = hn[:].bitcast(F32)
        hg_w = hg[:].bitcast(F32)

        def copy_on(eng, dst, src):
            if eng == "act":
                nc.scalar.copy(out=dst, in_=src)
            else:
                nc.vector.tensor_copy(out=dst, in_=src)

        def tr(dst, src, ident):
            return lambda: nc.tensor.transpose(dst, src, ident[:])

        def job_rows(src, dst):
            pt = tp.tile([P, 8, P], BF16, name="pt_f", tag="tp")
            ts = [tr(pt[:, t, :], src[:, t, :], ident_b) for t in range(8)]
            return ts, lambda eng: copy_on(eng, dst[:], pt[:].rearrange("p t b -> p (t b)"))

        def job_h(t):
            pt = tp.tile([P, 4, P], F32, name="pt_h", tag="tp")
            ts = [tr(pt[:, wb, :], hn_w[:, t, wb * P:(wb + 1) * P], ident_f) for wb in range(4)]
            return ts, lambda eng: copy_on(eng, hg_w[:, :, t * P:(t + 1) * P, :],
                                           pt[:].rearrange("p (g u) b -> p g b u", g=2))

        def begin_w(c):
            w = wt[c]
            w["w01"] = wpool.tile([P, 3, 2, 2], F32, name="w01", tag="w01")
            w["wit"] = wpool.tile([P, 15, P], BF16, name="wit", tag="wit")
            w["wg"] = wpool.tile([P, 6, 2, P, 4], BF16, name="wg", tag="wg", align_bytes=64)
            w["wc"] = wpool.tile([P, 6, 2, P], U32, name="wc", tag="wc", align_bytes=64)
            w["ws"] = wpool.tile([P, 6, 2, P], U8, name="ws", tag="ws", align_bytes=64)

        def small_w(c):
            win_v = wt[c]["win"][:].rearrange("p G (e k) -> p G e k", e=2)
            nc.scalar.copy(out=wt[c]["w01"][:], in_=win_v[:, :, :, 256:258])
            nc.scalar.copy(out=wx[:, c, 0:2, 0:2], in_=win_v[:, 0, :, 256:258])
            nc.scalar.copy(out=wx[:, c, 2, 0:2], in_=win_v[:, 2, 0, 256:258])

        def job_ia(c):
            win_v = wt[c]["win"][:].rearrange("p G (e k) -> p G e k", e=2)
            wit = wt[c]["wit"]
            pt = tp.tile([P, 8, P], BF16, name="pt_a", tag="tp")
            ts = [tr(pt[:, i, :], win_v[:, i // 4, (i // 2) % 2, (i % 2) * P:(i % 2 + 1) * P], ident_b)
                  for i in range(8)]
            return ts, lambda eng: copy_on(eng, wit[:, 0:8, :], pt[:])

        def job_ib(c):
            win_v = wt[c]["win"][:].rearrange("p G (e k) -> p G e k", e=2)
            wit = wt[c]["wit"]
            pt = tp.tile([P, 8, P], BF16, name="pt_b", tag="tp")
            ts = [tr(pt[:, i, :], win_v[:, 2, i // 2, (i % 2) * P:(i % 2 + 1) * P], ident_b) for i in range(4)]
            ts.extend([tr(pt[:, 4 + i, :], wx[:, c, i, :], ident_b) for i in range(3)])
            return ts, lambda eng: copy_on(eng, wit[:, 8:15, :], pt[:, 0:7, :])

        def job_w(c, ge):
            wn_w = wt[c]["wn"][:].bitcast(F32)
            wg_w = wt[c]["wg"][:].bitcast(F32)
            G, e = ge // 2, ge % 2
            pt = tp.tile([P, 4, P], F32, name="pt_w", tag="tp")
            ts = [tr(pt[:, wb, :], wn_w[:, G, e * 512 + wb * P:e * 512 + (wb + 1) * P], ident_f)
                  for wb in range(4)]
            return ts, lambda eng: copy_on(eng, wg_w[:, ge, :, :, :],
                                           pt[:].rearrange("p (g u) q -> p g q u", g=2))

        def quant_w(c, G):
            w = wt[c]
            nc.vector.quantize_mx(
                out=w["wc"][:, 2 * G:2 * G + 2, :, :].rearrange("p a g q -> p (a g q)").bitcast(FP8X4),
                scales=w["ws"][:, 2 * G:2 * G + 2, :, :].rearrange("p a g q -> p (a g q)"),
                in_=w["wg"][:, 2 * G:2 * G + 2, :, :, :].rearrange("p a g q t -> p (a g q t)"))

        def quant_h(g, bh):
            bs = slice(bh * NB, (bh + 1) * NB)
            nc.vector.quantize_mx(out=hc[:, g, bs].bitcast(FP8X4), scales=hs[:, g, bs],
                                  in_=hg[:, g, bs, :].rearrange("p b t -> p (b t)"))

        def job_o(c, i):
            f_t = ft[c]
            js = slice(256 * c, 256 * (c + 1))
            pt = tp.tile([P, 2, 2, P], F32, name="pt_o", tag="tp")
            ts = [tr(pt[:, k, e, :], f_t[:, e, (2 * i + k) * P:(2 * i + k + 1) * P], ident_f)
                  for k in range(2) for e in range(2)]

            def ev(eng):
                o_t = work.tile([P, 2, 256], F32, name="o_t", tag="o_t", bufs=3)
                nc.vector.tensor_tensor(out=o_t[:].rearrange("p k (q e) -> p k q e", e=2),
                                        in0=pt[:].rearrange("p k e q -> p k q e"),
                                        in1=hn[:, 2 * i:2 * i + 2, js].rearrange("p k (q e) -> p k q e", e=2),
                                        op=ALU.add)
                nc.sync.dma_start(out=out_v[:, 2 * i:2 * i + 2, js], in_=o_t[:])
            return ts, ev

        def run_job(job, eng):
            for t in job[0]:
                t()
            job[1](eng)

        begin_w(0)
        run_job(job_rows(fn, feat_t), "act")
        run_job(job_rows(an, aux_t), "dve")
        small_w(0)
        run_job(job_ia(0), "act")
        run_job(job_ib(0), "dve")
        run_job(job_rows(xn, x_t), "act")
        for t in range(4):
            run_job(job_h(t), "act" if t % 2 == 0 else "dve")
        for ge in range(6):
            run_job(job_w(0, ge), "act" if ge % 2 == 0 else "dve")
            if ge == 0:
                quant_h(0, 0)
                quant_h(1, 0)
            if ge == 3:
                quant_w(0, 0)
            if ge == 5:
                quant_w(0, 1)
        quant_w(0, 2)
        nc.vector.tensor_tensor(out=b_r[:], in0=bi[:, 0:4, :], in1=bh2[:, 0:4, :], op=ALU.add)
        nc.vector.scalar_tensor_tensor(out=b_zn[:], in0=bi[:, 4:8, :], scalar=-1.0, in1=bh2[:, 4:8, :],
                                       op0=ALU.mult, op1=ALU.subtract)
        nc.vector.tensor_copy(out=b_in[:], in_=bi[:, 8:12, :])
        nc.vector.tensor_copy(out=b_hn[:], in_=bh2[:, 8:12, :])


        def unit_of(s):
            return s // 4, (s // 2) % 2, s % 2

        def mm(ps, lhsT, rhs, start, stop):
            return lambda: nc.tensor.matmul(ps[:], lhsT=lhsT, rhs=rhs, start=start, stop=stop)

        def tacc(dst, src, stop):
            return lambda: nc.tensor.matmul(dst, lhsT=src, rhs=ident_f[:], is_transpose=True, start=False, stop=stop)

        def pe_ra(s):
            c, bh, e = unit_of(s)
            wc, ws = wt[c]["wc"], wt[c]["ws"]
            ps = acc.tile([P, 4, P], F32, name="gra", tag="acc")
            for i in range(4):
                cs = slice(bh * NB + i * P, bh * NB + (i + 1) * P)
                for kg in range(2):
                    nc.tensor.matmul_mx(ps[:, i, :], lhsT=hc[:, kg, cs].bitcast(FP8X4), lhsT_scale=hs[:, kg, cs],
                                        rhs=wc[:, e, kg, :].bitcast(FP8X4), rhs_scale=ws[:, e, kg, :],
                                        start=(kg == 0), stop=(kg == 1))
            ra[s] = work.tile([P, 4, P], F32, name="grs", tag="grs", bufs=2)
            return lambda: nc.scalar.copy(out=ra[s][:], in_=ps[:])

        def pe_unit(s, ts):
            c, bh, e = unit_of(s)
            w = wt[c]
            wit, wc, ws = w["wit"], w["wc"], w["ws"]
            bs = slice(bh * NB, (bh + 1) * NB)
            gi_r = acc.tile([P, NB], F32, name="gi_r", tag="acc")
            gi_z = acc.tile([P, NB], F32, name="gi_z", tag="acc")
            gi_n = acc.tile([P, NB], F32, name="gi_n", tag="acc")
            ms = [mm(gi_r, wit[:, 2 * e, :], feat_t[:, bs], True, False),
                  mm(gi_r, wit[:, 2 * e + 1, :], aux_t[:, bs], False, False),
                  mm(gi_r, wit[:, 12 + e, :], x_t[:, bs], False, False),
                  mm(gi_z, wit[:, 4 + 2 * e, :], feat_t[:, bs], True, False),
                  mm(gi_z, wit[:, 4 + 2 * e + 1, :], aux_t[:, bs], False, True),
                  mm(gi_n, wit[:, 8 + 2 * e, :], feat_t[:, bs], True, False),
                  mm(gi_n, wit[:, 8 + 2 * e + 1, :], aux_t[:, bs], False, e == 1)]
            if e == 0:
                ms.append(mm(gi_n, wit[:, 14, :], x_t[:, bs], False, True))
            grs = ra[s]
            late = [tacc(gi_r[:, i * P:(i + 1) * P], grs[:, i, :], i == 3) for i in range(4)]
            weave(ms, ts, late)
            gh = {}
            for G in (2, 1):
                ps = acc.tile([P, NB], F32, name="gh%d" % G, tag="acc")
                for kg in range(2):
                    nc.tensor.matmul_mx(ps[:], lhsT=wc[:, 2 * G + e, kg, :].bitcast(FP8X4),
                                        lhsT_scale=ws[:, 2 * G + e, kg, :],
                                        rhs=hc[:, kg, bs].bitcast(FP8X4), rhs_scale=hs[:, kg, bs],
                                        start=(kg == 0), stop=(kg == 1))
                gh[G] = ps
            ra_out = pe_ra(s + 1) if s + 1 < NSLOT else None
            if e == 0:
                pr[s // 2] = {"un": work.tile([P, 2, NB], F32, name="un", tag="un", bufs=4),
                              "uz": work.tile([P, 2, NB], F32, name="uz", tag="uz", bufs=4),
                              "vz": work.tile([P, 2, NB], F32, name="vz", tag="vz", bufs=2)}
            ut[s] = {"ra_out": ra_out, "gi_r": gi_r, "gi_n": gi_n, "gi_z": gi_z, "gh": gh,
                     "ar": work.tile([P, NB], F32, name="ar", tag="ar", bufs=2),
                     "qn": work.tile([P, NB], F32, name="qn", tag="qn", bufs=3)}

        def stt(dst, in0, scalar, in1, op0, op1):
            nc.vector.scalar_tensor_tensor(out=dst, in0=in0, scalar=scalar, in1=in1, op0=op0, op1=op1)

        def tt(eng, dst, in0, in1, op):
            if eng == "dve":
                nc.vector.tensor_tensor(out=dst, in0=in0, in1=in1, op=op)
            else:
                nc.gpsimd.tensor_tensor(out=dst, in0=in0, in1=in1, op=op)

        def h_t(p, i):
            c, bh = p // 2, p % 2
            return hg[:, c // 2, bh * NB:(bh + 1) * NB, 2 * (c % 2) + i]

        def sub_h(eng, p, lo, hi):
            un = pr[p]["un"]
            for i in range(lo, hi):
                tt(eng, un[:, i, :], un[:, i, :], h_t(p, i), ALU.subtract)

        def mul_z(eng, p, lo, hi):
            c, bh = p // 2, p % 2
            if c not in ft:
                ft[c] = work.tile([P, 2, B], F32, name="f_t", tag="f_t", bufs=2)
            for i in range(lo, hi):
                tt(eng, ft[c][:, i, bh * NB:(bh + 1) * NB], pr[p]["uz"][:, i, :], pr[p]["un"][:, i, :], ALU.mult)

        def prep_jobs(s):
            c, k = s // 4 + 1, s % 4
            if c > 3:
                return []
            seq = [("w", c, ge) for ge in range(6)] + [("ia", c, 0), ("ib", c, 0)]
            cuts = (0, 0, 3, 6, 8) if c == 1 else (0, 2, 4, 6, 8)
            return seq[cuts[k]:cuts[k + 1]]

        def make_job(d):
            if d[0] == "w":
                if d[2] == 0:
                    begin_w(d[1])
                return job_w(d[1], d[2])
            if d[0] == "ia":
                return job_ia(d[1])
            if d[0] == "ib":
                return job_ib(d[1])
            return job_o(d[1], d[2])

        def slot(s):
            c, bh, e = unit_of(s)
            k = s % 4
            p = s // 2
            main = s < NSLOT
            if main and k == 0 and c + 2 < 4:
                load_w(c + 2)
            jobs = [make_job(d) for d in prep_jobs(s)] if main else []
            ojobs = [job_o(co, io) for co, io in O_AT.get(s, [])]
            ts = []
            for j in jobs + ojobs:
                ts.extend(j[0])
            if main:
                pe_unit(s, ts)
                u = ut[s]
                pp = pr[p]
                w01 = wt[c]["w01"]
                bs = slice(bh * NB, (bh + 1) * NB)
                x0 = xb_v[:, bs, 0]
                x1 = xb_v[:, bs, 1]
                un = pp["un"][:, e, :]
                uz = pp["uz"][:, e, :]
                vz = pp["vz"][:, e, :]
                ar = u["ar"]
                nc.scalar.activation(out=ar[:], in_=u["gi_r"][:], func=AF.Sigmoid, bias=b_r[:, c, e:e + 1], scale=1.0)
                for j in jobs:
                    j[1]("act")
                if u["ra_out"] is not None:
                    u["ra_out"]()
                if c + 1 < 4 and k == 2:
                    small_w(c + 1)
                for d in prep_jobs(s - 1) if s > 0 else []:
                    if d[0] == "w" and d[2] % 2 == 1:
                        quant_w(d[1], d[2] // 2)
                stt(uz, x0, w01[:, 1, e, 0:1], u["gi_z"][:], ALU.mult, ALU.add)
                if e == 1:
                    stt(un, x0, w01[:, 2, e, 0:1], u["gi_n"][:], ALU.mult, ALU.add)
                if e == 1:
                    stt(un, x1, w01[:, 2, e, 1:2], un, ALU.mult, ALU.add)
                stt(u["qn"][:], u["gh"][2][:], b_hn[:, c, e:e + 1], ar[:], ALU.add, ALU.mult)
                if e == 0:
                    tt("dve", un, u["gi_n"][:], u["qn"][:], ALU.add)
                stt(vz, x1, w01[:, 1, e, 1:2], u["gh"][1][:], ALU.mult, ALU.add)
                for j in ojobs:
                    j[1]("dve")
                if p >= PD:
                    if e == 1:
                        tt("dve", un, un, u["qn"][:], ALU.add)
                    tt("dve", uz, uz, vz, ALU.add)
            else:
                for t in ts:
                    t()
                for j in ojobs:
                    j[1]("dve")
            if 1 <= s <= NSLOT:
                tanh_of(s - 1)
                if (s - 1) // 2 >= PD:
                    sig_z(s - 1)
                elif s % 2 == 0:
                    sig_z(s - 2)
                    sig_z(s - 1)
            if main and s % 2 == 1 and p < PD:
                tt("pool", un, un, u["qn"][:], ALU.add)
                tt("pool", pp["uz"][:], pp["uz"][:], pp["vz"][:], ALU.add)
            if s % 2 == 1 and 1 <= p <= PD:
                mul_z("pool", p - 1, 0, 2)
            if s % 2 == 0 and 1 <= p <= LASTP:
                sub_h("pool", p - 1, 0, 2)
                if p - 1 >= PD:
                    mul_z("pool", p - 1, 0, 2)
            if s == NSLOT - 1:
                sub_h("pool", LASTP, 0, 1)
                mul_z("pool", LASTP, 0, 1)
            if s == NSLOT:
                sub_h("dve", LASTP, 1, 2)
                mul_z("dve", LASTP, 1, 2)

        def tanh_of(s):
            c1, bh1, e1 = unit_of(s)
            un1 = pr[s // 2]["un"][:, e1, :]
            nc.scalar.activation(out=un1, in_=un1, func=AF.Tanh, bias=b_in[:, c1, e1:e1 + 1], scale=1.0)

        def sig_z(s):
            c1, bh1, e1 = unit_of(s)
            uz1 = pr[s // 2]["uz"][:, e1, :]
            nc.scalar.activation(out=uz1, in_=uz1, func=AF.Sigmoid, bias=b_zn[:, c1, e1:e1 + 1], scale=-1.0)

        pe_ra(0)()
        for s in range(NSLOT + 2):
            slot(s)
            if s == 0:
                for t in range(4, 8):
                    run_job(job_h(t), "act" if t % 2 == 0 else "dve")
                quant_h(0, 1)
                quant_h(1, 1)
